import numpy as np
import ml_dtypes

BF16 = ml_dtypes.bfloat16


def bf(x):
    return np.asarray(x, np.float32).astype(BF16)


def f32(x):
    return np.asarray(x, np.float32)


def f64(x):
    return np.asarray(x).astype(np.float64)


def striped(idx):
    return np.tile(idx.reshape(-1, 16).T, (8, 1))


C, S, N = 512, 4096, 1024
CURV = 0.25
SQRT_CURV = np.sqrt(CURV)
MAX_NORM = 1.0 - 1e-3
R_LO, R_HI = 0.3, 2.0


def setup_inputs():
    radii = np.random.uniform(R_LO, R_HI, (1, S))
    x = f32(np.random.standard_normal((C, S)) * radii / np.sqrt(C))
    return {"x": x, "offs": striped(np.random.permutation(S)[:N])}


def reference(x, offs):
    idx = offs[:16].T.reshape(-1)
    v = f64(x)[:, idx]
    r = np.sqrt(np.sum(v * v, axis=0, keepdims=True))
    t = np.tanh(SQRT_CURV * r) / SQRT_CURV
    return v * (np.minimum(t, MAX_NORM) / r)

@@ -1,0 +1,65 @@
+import concourse.mybir as mybir
+
+C, S, N = 512, 4096, 1024
+P = 128
+BLOCKS = C // P
+BANK = 512
+HALVES = N // BANK
+SQRT_CURV = 0.5
+MAX_NORM = 0.999
+FLOPS = 2 * C * N
+
+F32, BF16, U16 = mybir.dt.float32, mybir.dt.bfloat16, mybir.dt.uint16
+MULT, MIN = mybir.AluOpType.mult, mybir.AluOpType.min
+COPY = mybir.ActivationFunctionType.Copy
+TANH = mybir.ActivationFunctionType.Tanh
+INV_SQRT = mybir.ActivationFunctionType.Abs_reciprocal_sqrt
+
+
+def tile_poincarehead_kernel(tc, x, offs, out):
+    nc = tc.nc
+    x_blocks = x.rearrange("(b p) s -> b p s", p=P)
+    out_blocks = out.rearrange("(b p) n -> b p n", p=P)
+    with (
+        tc.tile_pool(name="held", bufs=1) as held,
+        tc.psum_pool(name="psum", bufs=1) as psum,
+    ):
+        offsets = held.tile([P, N // 16], U16, name="offsets")
+        nc.sync.dma_start(offsets[:], offs)
+        tables = [held.tile([P, S], F32, name=f"table{b}") for b in range(BLOCKS)]
+        for b in range(BLOCKS):
+            nc.sync.dma_start(tables[b][:], x_blocks[b, :, :])
+
+        ones = held.tile([P, P], BF16, name="ones")
+        nc.vector.memset(ones[:], 1.0)
+
+        picked = [held.tile([P, N], F32, name=f"picked{b}") for b in range(BLOCKS)]
+        squares = [held.tile([P, N], BF16, name=f"squares{b}") for b in range(BLOCKS)]
+        norm_sq = [psum.tile([P, BANK], F32, name=f"norm_sq{h}") for h in range(HALVES)]
+        for b in range(BLOCKS):
+            nc.scalar.activation(picked[b][:], tables[b][:].indirect(offsets[:]), COPY)
+            nc.vector.tensor_tensor(squares[b][:], picked[b][:], picked[b][:], MULT)
+            for h in range(HALVES):
+                nc.tensor.matmul(
+                    norm_sq[h][:],
+                    ones[:],
+                    squares[b][:, h * BANK : (h + 1) * BANK],
+                    start=(b == 0),
+                    stop=(b == BLOCKS - 1),
+                )
+
+        inv_a = [held.tile([P, BANK], F32, name=f"inv_a{h}") for h in range(HALVES)]
+        a = [held.tile([P, BANK], F32, name=f"a{h}") for h in range(HALVES)]
+        tanh_a = [held.tile([P, BANK], F32, name=f"tanh_a{h}") for h in range(HALVES)]
+        factor = [held.tile([P, BANK], F32, name=f"factor{h}") for h in range(HALVES)]
+        mapped = [held.tile([P, N], F32, name=f"mapped{b}") for b in range(BLOCKS)]
+        for h in range(HALVES):
+            nc.scalar.activation(inv_a[h][:], norm_sq[h][:], INV_SQRT, scale=SQRT_CURV * SQRT_CURV)
+            nc.vector.scalar_tensor_tensor(a[h][:], norm_sq[h][:], SQRT_CURV * SQRT_CURV, inv_a[h][:], MULT, MULT)
+        for h in range(HALVES):
+            cols = slice(h * BANK, (h + 1) * BANK)
+            nc.scalar.activation(tanh_a[h][:], a[h][:], TANH)
+            nc.vector.scalar_tensor_tensor(factor[h][:], tanh_a[h][:], SQRT_CURV * MAX_NORM, inv_a[h][:], MIN, MULT)
+            for b in range(BLOCKS):
+                nc.vector.tensor_tensor(mapped[b][:, cols], picked[b][:, cols], factor[h][:], MULT)
+                nc.sync.dma_start(out_blocks[b, :, cols], mapped[b][:, cols])

@@ -33,20 +33,21 @@ def tile_poincarehead_kernel(tc, x, offs, out):
         ones = held.tile([P, P], BF16, name="ones")
         nc.vector.memset(ones[:], 1.0)
 
+        scratch = held.tile([P, 1], F32, name="scratch")
+        warmed = held.tile([P, 1], F32, name="warmed")
+        nc.vector.memset(scratch[:], 1.0)
+        nc.scalar.activation(warmed[:], scratch[:], INV_SQRT)
+
         picked = [held.tile([P, N], F32, name=f"picked{b}") for b in range(BLOCKS)]
         squares = [held.tile([P, N], BF16, name=f"squares{b}") for b in range(BLOCKS)]
         norm_sq = [psum.tile([P, BANK], F32, name=f"norm_sq{h}") for h in range(HALVES)]
         for b in range(BLOCKS):
-            nc.scalar.activation(picked[b][:], tables[b][:].indirect(offsets[:]), COPY)
-            nc.vector.tensor_tensor(squares[b][:], picked[b][:], picked[b][:], MULT)
             for h in range(HALVES):
-                nc.tensor.matmul(
-                    norm_sq[h][:],
-                    ones[:],
-                    squares[b][:, h * BANK : (h + 1) * BANK],
-                    start=(b == 0),
-                    stop=(b == BLOCKS - 1),
-                )
+                cols = slice(h * BANK, (h + 1) * BANK)
+                half_list = offsets[:, h * (BANK // 16) : (h + 1) * (BANK // 16)]
+                nc.scalar.activation(picked[b][:, cols], tables[b][:].indirect(half_list), COPY)
+                nc.vector.tensor_tensor(squares[b][:, cols], picked[b][:, cols], picked[b][:, cols], MULT)
+                nc.tensor.matmul(norm_sq[h][:], ones[:], squares[b][:, cols], start=(b == 0), stop=(b == BLOCKS - 1))
 
         inv_a = [held.tile([P, BANK], F32, name=f"inv_a{h}") for h in range(HALVES)]
         a = [held.tile([P, BANK], F32, name=f"a{h}") for h in range(HALVES)]

@@ -61,6 +61,8 @@ def tile_poincarehead_kernel(tc, x, offs, out):
             cols = slice(h * BANK, (h + 1) * BANK)
             nc.scalar.activation(tanh_a[h][:], a[h][:], TANH)
             nc.vector.scalar_tensor_tensor(factor[h][:], tanh_a[h][:], SQRT_CURV * MAX_NORM, inv_a[h][:], MIN, MULT)
-            for b in range(BLOCKS):
+            nc.gpsimd.tensor_tensor(mapped[BLOCKS - 1][:, cols], picked[BLOCKS - 1][:, cols], factor[h][:], MULT)
+            for b in range(BLOCKS - 1):
                 nc.vector.tensor_tensor(mapped[b][:, cols], picked[b][:, cols], factor[h][:], MULT)
+            for b in range(BLOCKS):
                 nc.sync.dma_start(out_blocks[b, :, cols], mapped[b][:, cols])

@@ -52,17 +52,24 @@ def tile_poincarehead_kernel(tc, x, offs, out):
         inv_a = [held.tile([P, BANK], F32, name=f"inv_a{h}") for h in range(HALVES)]
         a = [held.tile([P, BANK], F32, name=f"a{h}") for h in range(HALVES)]
         tanh_a = [held.tile([P, BANK], F32, name=f"tanh_a{h}") for h in range(HALVES)]
-        factor = [held.tile([P, BANK], F32, name=f"factor{h}") for h in range(HALVES)]
+        factor = held.tile([P, BANK], F32, name="factor")
         mapped = [held.tile([P, N], F32, name=f"mapped{b}") for b in range(BLOCKS)]
         for h in range(HALVES):
             nc.scalar.activation(inv_a[h][:], norm_sq[h][:], INV_SQRT, scale=SQRT_CURV * SQRT_CURV)
             nc.vector.scalar_tensor_tensor(a[h][:], norm_sq[h][:], SQRT_CURV * SQRT_CURV, inv_a[h][:], MULT, MULT)
-        for h in range(HALVES):
-            cols = slice(h * BANK, (h + 1) * BANK)
-            nc.scalar.activation(tanh_a[h][:], a[h][:], TANH)
-            nc.vector.scalar_tensor_tensor(factor[h][:], tanh_a[h][:], SQRT_CURV * MAX_NORM, inv_a[h][:], MIN, MULT)
-            nc.gpsimd.tensor_tensor(mapped[BLOCKS - 1][:, cols], picked[BLOCKS - 1][:, cols], factor[h][:], MULT)
-            for b in range(BLOCKS - 1):
-                nc.vector.tensor_tensor(mapped[b][:, cols], picked[b][:, cols], factor[h][:], MULT)
-            for b in range(BLOCKS):
-                nc.sync.dma_start(out_blocks[b, :, cols], mapped[b][:, cols])
+
+        cols = slice(0, BANK)
+        over_a = [held.tile([P, BANK], F32, name=f"over_a{b}") for b in range(BLOCKS)]
+        for b in range(BLOCKS):
+            nc.vector.tensor_tensor(over_a[b][:], picked[b][:, cols], inv_a[0][:], MULT)
+        nc.scalar.activation(tanh_a[0][:], a[0][:], TANH)
+        for b in range(BLOCKS):
+            nc.vector.scalar_tensor_tensor(mapped[b][:, cols], tanh_a[0][:], SQRT_CURV * MAX_NORM, over_a[b][:], MIN, MULT)
+            nc.sync.dma_start(out_blocks[b, :, cols], mapped[b][:, cols])
+
+        cols = slice(BANK, N)
+        nc.scalar.activation(tanh_a[1][:], a[1][:], TANH)
+        nc.vector.scalar_tensor_tensor(factor[:], tanh_a[1][:], SQRT_CURV * MAX_NORM, inv_a[1][:], MIN, MULT)
+        for b in range(BLOCKS):
+            nc.vector.tensor_tensor(mapped[b][:, cols], picked[b][:, cols], factor[:], MULT)
+            nc.sync.dma_start(out_blocks[b, :, cols], mapped[b][:, cols])

@@ -25,10 +25,11 @@ def tile_poincarehead_kernel(tc, x, offs, out):
         tc.psum_pool(name="psum", bufs=1) as psum,
     ):
         offsets = held.tile([P, N // 16], U16, name="offsets")
-        nc.sync.dma_start(offsets[:], offs)
         tables = [held.tile([P, S], F32, name=f"table{b}") for b in range(BLOCKS)]
         for b in range(BLOCKS):
             nc.sync.dma_start(tables[b][:], x_blocks[b, :, :])
+            if b == 0:
+                nc.sync.dma_start(offsets[:], offs)
 
         ones = held.tile([P, P], BF16, name="ones")
         nc.vector.memset(ones[:], 1.0)
@@ -42,12 +43,20 @@ def tile_poincarehead_kernel(tc, x, offs, out):
         squares = [held.tile([P, N], BF16, name=f"squares{b}") for b in range(BLOCKS)]
         norm_sq = [psum.tile([P, BANK], F32, name=f"norm_sq{h}") for h in range(HALVES)]
         for b in range(BLOCKS):
-            for h in range(HALVES):
-                cols = slice(h * BANK, (h + 1) * BANK)
-                half_list = offsets[:, h * (BANK // 16) : (h + 1) * (BANK // 16)]
-                nc.scalar.activation(picked[b][:, cols], tables[b][:].indirect(half_list), COPY)
+            width = BANK if b < BLOCKS - 1 else BANK // 2
+            for first in range(0, N, width):
+                cols = slice(first, first + width)
+                h, in_bank = divmod(first, BANK)
+                piece_list = offsets[:, first // 16 : (first + width) // 16]
+                nc.scalar.activation(picked[b][:, cols], tables[b][:].indirect(piece_list), COPY)
                 nc.vector.tensor_tensor(squares[b][:, cols], picked[b][:, cols], picked[b][:, cols], MULT)
-                nc.tensor.matmul(norm_sq[h][:], ones[:], squares[b][:, cols], start=(b == 0), stop=(b == BLOCKS - 1))
+                nc.tensor.matmul(
+                    norm_sq[h][:, in_bank : in_bank + width],
+                    ones[:],
+                    squares[b][:, cols],
+                    start=(b == 0),
+                    stop=(b == BLOCKS - 1 and in_bank + width == BANK),
+                )
 
         inv_a = [held.tile([P, BANK], F32, name=f"inv_a{h}") for h in range(HALVES)]
         a = [held.tile([P, BANK], F32, name=f"a{h}") for h in range(HALVES)]

@@ -4,7 +4,7 @@ C, S, N = 512, 4096, 1024
 P = 128
 BLOCKS = C // P
 BANK = 512
-HALVES = N // BANK
+SUMS = ((0, BANK), (BANK, N - BANK // 4), (N - BANK // 4, N))
 SQRT_CURV = 0.5
 MAX_NORM = 0.999
 FLOPS = 2 * C * N
@@ -41,44 +41,45 @@ def tile_poincarehead_kernel(tc, x, offs, out):
 
         picked = [held.tile([P, N], F32, name=f"picked{b}") for b in range(BLOCKS)]
         squares = [held.tile([P, N], BF16, name=f"squares{b}") for b in range(BLOCKS)]
-        norm_sq = [psum.tile([P, BANK], F32, name=f"norm_sq{h}") for h in range(HALVES)]
+        norm_sq = [psum.tile([P, end - first], F32, name=f"norm_sq{k}") for k, (first, end) in enumerate(SUMS)]
         for b in range(BLOCKS):
-            width = BANK if b < BLOCKS - 1 else BANK // 2
-            for first in range(0, N, width):
-                cols = slice(first, first + width)
-                h, in_bank = divmod(first, BANK)
-                piece_list = offsets[:, first // 16 : (first + width) // 16]
-                nc.scalar.activation(picked[b][:, cols], tables[b][:].indirect(piece_list), COPY)
-                nc.vector.tensor_tensor(squares[b][:, cols], picked[b][:, cols], picked[b][:, cols], MULT)
-                nc.tensor.matmul(
-                    norm_sq[h][:, in_bank : in_bank + width],
-                    ones[:],
-                    squares[b][:, cols],
-                    start=(b == 0),
-                    stop=(b == BLOCKS - 1 and in_bank + width == BANK),
-                )
+            step = BANK if b < BLOCKS - 1 else BANK // 2
+            for k, (first, end) in enumerate(SUMS):
+                for lo in range(first, end, step):
+                    hi = min(lo + step, end)
+                    cols = slice(lo, hi)
+                    nc.scalar.activation(picked[b][:, cols], tables[b][:].indirect(offsets[:, lo // 16 : hi // 16]), COPY)
+                    nc.vector.tensor_tensor(squares[b][:, cols], picked[b][:, cols], picked[b][:, cols], MULT)
+                    nc.tensor.matmul(
+                        norm_sq[k][:, lo - first : hi - first],
+                        ones[:],
+                        squares[b][:, cols],
+                        start=(b == 0),
+                        stop=(b == BLOCKS - 1 and hi == end),
+                    )
 
-        inv_a = [held.tile([P, BANK], F32, name=f"inv_a{h}") for h in range(HALVES)]
-        a = [held.tile([P, BANK], F32, name=f"a{h}") for h in range(HALVES)]
-        tanh_a = [held.tile([P, BANK], F32, name=f"tanh_a{h}") for h in range(HALVES)]
+        inv_a = held.tile([P, N], F32, name="inv_a")
+        a = held.tile([P, N], F32, name="a")
+        tanh_a = held.tile([P, N], F32, name="tanh_a")
         factor = held.tile([P, BANK], F32, name="factor")
         mapped = [held.tile([P, N], F32, name=f"mapped{b}") for b in range(BLOCKS)]
-        for h in range(HALVES):
-            nc.scalar.activation(inv_a[h][:], norm_sq[h][:], INV_SQRT, scale=SQRT_CURV * SQRT_CURV)
-            nc.vector.scalar_tensor_tensor(a[h][:], norm_sq[h][:], SQRT_CURV * SQRT_CURV, inv_a[h][:], MULT, MULT)
+        for k, (first, end) in enumerate(SUMS):
+            cols = slice(first, end)
+            nc.scalar.activation(inv_a[:, cols], norm_sq[k][:], INV_SQRT, scale=SQRT_CURV * SQRT_CURV)
+            nc.vector.scalar_tensor_tensor(a[:, cols], norm_sq[k][:], SQRT_CURV * SQRT_CURV, inv_a[:, cols], MULT, MULT)
 
         cols = slice(0, BANK)
         over_a = [held.tile([P, BANK], F32, name=f"over_a{b}") for b in range(BLOCKS)]
         for b in range(BLOCKS):
-            nc.vector.tensor_tensor(over_a[b][:], picked[b][:, cols], inv_a[0][:], MULT)
-        nc.scalar.activation(tanh_a[0][:], a[0][:], TANH)
+            nc.vector.tensor_tensor(over_a[b][:], picked[b][:, cols], inv_a[:, cols], MULT)
+        nc.scalar.activation(tanh_a[:, cols], a[:, cols], TANH)
         for b in range(BLOCKS):
-            nc.vector.scalar_tensor_tensor(mapped[b][:, cols], tanh_a[0][:], SQRT_CURV * MAX_NORM, over_a[b][:], MIN, MULT)
+            nc.vector.scalar_tensor_tensor(mapped[b][:, cols], tanh_a[:, cols], SQRT_CURV * MAX_NORM, over_a[b][:], MIN, MULT)
             nc.sync.dma_start(out_blocks[b, :, cols], mapped[b][:, cols])
 
         cols = slice(BANK, N)
-        nc.scalar.activation(tanh_a[1][:], a[1][:], TANH)
-        nc.vector.scalar_tensor_tensor(factor[:], tanh_a[1][:], SQRT_CURV * MAX_NORM, inv_a[1][:], MIN, MULT)
+        nc.scalar.activation(tanh_a[:, cols], a[:, cols], TANH)
+        nc.vector.scalar_tensor_tensor(factor[:], tanh_a[:, cols], SQRT_CURV * MAX_NORM, inv_a[:, cols], MIN, MULT)
         for b in range(BLOCKS):
             nc.vector.tensor_tensor(mapped[b][:, cols], picked[b][:, cols], factor[:], MULT)
             nc.sync.dma_start(out_blocks[b, :, cols], mapped[b][:, cols])

@@ -5,6 +5,7 @@ P = 128
 BLOCKS = C // P
 BANK = 512
 SUMS = ((0, BANK), (BANK, N - BANK // 4), (N - BANK // 4, N))
+EARLY = 384
 SQRT_CURV = 0.5
 MAX_NORM = 0.999
 FLOPS = 2 * C * N
@@ -61,15 +62,15 @@ def tile_poincarehead_kernel(tc, x, offs, out):
         inv_a = held.tile([P, N], F32, name="inv_a")
         a = held.tile([P, N], F32, name="a")
         tanh_a = held.tile([P, N], F32, name="tanh_a")
-        factor = held.tile([P, BANK], F32, name="factor")
+        factor = held.tile([P, N - EARLY], F32, name="factor")
         mapped = [held.tile([P, N], F32, name=f"mapped{b}") for b in range(BLOCKS)]
         for k, (first, end) in enumerate(SUMS):
             cols = slice(first, end)
             nc.scalar.activation(inv_a[:, cols], norm_sq[k][:], INV_SQRT, scale=SQRT_CURV * SQRT_CURV)
             nc.vector.scalar_tensor_tensor(a[:, cols], norm_sq[k][:], SQRT_CURV * SQRT_CURV, inv_a[:, cols], MULT, MULT)
 
-        cols = slice(0, BANK)
-        over_a = [held.tile([P, BANK], F32, name=f"over_a{b}") for b in range(BLOCKS)]
+        cols = slice(0, EARLY)
+        over_a = [held.tile([P, EARLY], F32, name=f"over_a{b}") for b in range(BLOCKS)]
         for b in range(BLOCKS):
             nc.vector.tensor_tensor(over_a[b][:], picked[b][:, cols], inv_a[:, cols], MULT)
         nc.scalar.activation(tanh_a[:, cols], a[:, cols], TANH)
@@ -77,7 +78,7 @@ def tile_poincarehead_kernel(tc, x, offs, out):
             nc.vector.scalar_tensor_tensor(mapped[b][:, cols], tanh_a[:, cols], SQRT_CURV * MAX_NORM, over_a[b][:], MIN, MULT)
             nc.sync.dma_start(out_blocks[b, :, cols], mapped[b][:, cols])
 
-        cols = slice(BANK, N)
+        cols = slice(EARLY, N)
         nc.scalar.activation(tanh_a[:, cols], a[:, cols], TANH)
         nc.vector.scalar_tensor_tensor(factor[:], tanh_a[:, cols], SQRT_CURV * MAX_NORM, inv_a[:, cols], MIN, MULT)
         for b in range(BLOCKS):

import concourse.mybir as mybir

C, S, N = 512, 4096, 1024
P = 128
BLOCKS = C // P
BANK = 512
SUMS = ((0, BANK), (BANK, N - BANK // 4), (N - BANK // 4, N))
EARLY = 384
SQRT_CURV = 0.5
MAX_NORM = 0.999
FLOPS = 2 * C * N

F32, BF16, U16 = mybir.dt.float32, mybir.dt.bfloat16, mybir.dt.uint16
MULT, MIN = mybir.AluOpType.mult, mybir.AluOpType.min
COPY = mybir.ActivationFunctionType.Copy
TANH = mybir.ActivationFunctionType.Tanh
INV_SQRT = mybir.ActivationFunctionType.Abs_reciprocal_sqrt


def tile_poincarehead_kernel(tc, x, offs, out):
    nc = tc.nc
    x_blocks = x.rearrange("(b p) s -> b p s", p=P)
    out_blocks = out.rearrange("(b p) n -> b p n", p=P)
    with (
        tc.tile_pool(name="held", bufs=1) as held,
        tc.psum_pool(name="psum", bufs=1) as psum,
    ):
        offsets = held.tile([P, N // 16], U16, name="offsets")
        tables = [held.tile([P, S], F32, name=f"table{b}") for b in range(BLOCKS)]
        for b in range(BLOCKS):
            nc.sync.dma_start(tables[b][:], x_blocks[b, :, :])
            if b == 0:
                nc.sync.dma_start(offsets[:], offs)

        ones = held.tile([P, P], BF16, name="ones")
        nc.vector.memset(ones[:], 1.0)

        scratch = held.tile([P, 1], F32, name="scratch")
        warmed = held.tile([P, 1], F32, name="warmed")
        nc.vector.memset(scratch[:], 1.0)
        nc.scalar.activation(warmed[:], scratch[:], INV_SQRT)

        picked = [held.tile([P, N], F32, name=f"picked{b}") for b in range(BLOCKS)]
        squares = [held.tile([P, N], BF16, name=f"squares{b}") for b in range(BLOCKS)]
        norm_sq = [psum.tile([P, end - first], F32, name=f"norm_sq{k}") for k, (first, end) in enumerate(SUMS)]
        for b in range(BLOCKS):
            step = BANK if b < BLOCKS - 1 else BANK // 2
            for k, (first, end) in enumerate(SUMS):
                for lo in range(first, end, step):
                    hi = min(lo + step, end)
                    cols = slice(lo, hi)
                    nc.scalar.activation(picked[b][:, cols], tables[b][:].indirect(offsets[:, lo // 16 : hi // 16]), COPY)
                    nc.vector.tensor_tensor(squares[b][:, cols], picked[b][:, cols], picked[b][:, cols], MULT)
                    nc.tensor.matmul(
                        norm_sq[k][:, lo - first : hi - first],
                        ones[:],
                        squares[b][:, cols],
                        start=(b == 0),
                        stop=(b == BLOCKS - 1 and hi == end),
                    )

        inv_a = held.tile([P, N], F32, name="inv_a")
        a = held.tile([P, N], F32, name="a")
        tanh_a = held.tile([P, N], F32, name="tanh_a")
        factor = held.tile([P, N - EARLY], F32, name="factor")
        mapped = [held.tile([P, N], F32, name=f"mapped{b}") for b in range(BLOCKS)]
        for k, (first, end) in enumerate(SUMS):
            cols = slice(first, end)
            nc.scalar.activation(inv_a[:, cols], norm_sq[k][:], INV_SQRT, scale=SQRT_CURV * SQRT_CURV)
            nc.vector.scalar_tensor_tensor(a[:, cols], norm_sq[k][:], SQRT_CURV * SQRT_CURV, inv_a[:, cols], MULT, MULT)

        cols = slice(0, EARLY)
        over_a = [held.tile([P, EARLY], F32, name=f"over_a{b}") for b in range(BLOCKS)]
        for b in range(BLOCKS):
            nc.vector.tensor_tensor(over_a[b][:], picked[b][:, cols], inv_a[:, cols], MULT)
        nc.scalar.activation(tanh_a[:, cols], a[:, cols], TANH)
        for b in range(BLOCKS):
            nc.vector.scalar_tensor_tensor(mapped[b][:, cols], tanh_a[:, cols], SQRT_CURV * MAX_NORM, over_a[b][:], MIN, MULT)
            nc.sync.dma_start(out_blocks[b, :, cols], mapped[b][:, cols])

        cols = slice(EARLY, N)
        nc.scalar.activation(tanh_a[:, cols], a[:, cols], TANH)
        nc.vector.scalar_tensor_tensor(factor[:], tanh_a[:, cols], SQRT_CURV * MAX_NORM, inv_a[:, cols], MIN, MULT)
        for b in range(BLOCKS):
            nc.vector.tensor_tensor(mapped[b][:, cols], picked[b][:, cols], factor[:], MULT)
            nc.sync.dma_start(out_blocks[b, :, cols], mapped[b][:, cols])
